import numpy as np
import ml_dtypes


def mxq(x, axis, fmt="e4m3"):
    dtype, down = {"e4m3": (ml_dtypes.float8_e4m3fn, 7), "e5m2": (ml_dtypes.float8_e5m2, 14)}[fmt]
    v = np.moveaxis(np.asarray(x, np.float32).astype(ml_dtypes.bfloat16).astype(np.float64), axis, -1)
    blocks = v.reshape(v.shape[:-1] + (-1, 32))
    amax = np.abs(blocks).max(-1, keepdims=True)
    byte = np.maximum(np.where(amax > 0, np.frexp(amax)[1] - 1 + 127, 0) - down, 1)
    scale = np.exp2(byte - 127.0)
    codes = (blocks / scale).astype(np.float32).astype(dtype).astype(np.float64)
    return np.moveaxis((codes * scale).reshape(v.shape), -1, axis)


WIDE = False


def mx_kscale(k):
    if not WIDE:
        return np.ones(k)
    levels = np.array([10, -10, 5, -5, 0])
    a = np.random.permutation(np.resize(levels, k // 512 * 4)).reshape(k // 512, 4)
    idx = np.arange(k)
    return np.exp2(a[idx // 512, idx % 128 // 32])


BF16 = ml_dtypes.bfloat16


def bf(x):
    return np.asarray(x, np.float32).astype(BF16)


def f64(x):
    return np.asarray(x).astype(np.float64)


N, IN_F, OUT_F = 1024, 512, 512
POW = 2


def setup_inputs():
    s = mx_kscale(IN_F)
    u = np.exp2(np.round(np.log2(mx_kscale(N)) / 2))
    return {"input": bf(np.random.standard_normal((N, IN_F)) * s / (u * u)[:, None]),
            "adj": bf(np.random.uniform(0.0, 1.0, (N, N)) * 1.5 / N ** 0.25 * u),
            "weight": bf(np.random.uniform(-1.0, 1.0, (IN_F, OUT_F)) * 1.7 / np.sqrt(IN_F) / s[:, None]),
            "bias": bf(np.random.standard_normal(OUT_F) * 0.3)}


def reference(input, adj, weight, bias):
    k_adj = f64(adj) ** POW
    support = mxq(f64(input), 1, "e4m3") @ mxq(f64(weight), 0, "e4m3")
    out = (mxq(k_adj, 1, "e4m3") @ mxq(support, 0, "e4m3")) + f64(bias)
    return np.where(out > 0, out, np.expm1(out))

@@ -1,0 +1,176 @@
+from contextlib import ExitStack
+
+import concourse.mybir as mybir
+from concourse.masks import make_identity
+
+F32 = mybir.dt.float32
+BF16 = mybir.dt.bfloat16
+U32 = mybir.dt.uint32
+U8 = mybir.dt.uint8
+I32 = mybir.dt.int32
+FP8X4 = mybir.dt.float8_e4m3fn_x4
+ALU = mybir.AluOpType
+ACT = mybir.ActivationFunctionType
+
+P = 128
+NODES = 1024
+IN_F = 512
+OUT_F = 512
+FLOPS = 2 * NODES * IN_F * OUT_F + 2 * NODES * NODES * OUT_F
+
+
+def tile_netgraphconvolution_kernel(tc, x_in, adj, weight, bias, out):
+    nc = tc.nc
+    with ExitStack() as ctx:
+        keep = ctx.enter_context(tc.tile_pool(name="keep", bufs=1))
+        ps_t = ctx.enter_context(tc.psum_pool(name="ps_t", bufs=3))
+        ps_s = ctx.enter_context(tc.psum_pool(name="ps_s", bufs=2))
+        ps_o = ctx.enter_context(tc.psum_pool(name="ps_o", bufs=3))
+
+        ident = keep.tile([P, P], F32, name="ident")
+        make_identity(nc, ident[:])
+        warm = keep.tile([P, 1], F32, name="warm")
+        nc.vector.memset(warm[:], 0.0)
+        nc.scalar.activation(out=warm[:], in_=warm[:], func=ACT.Exp)
+        ones = keep.tile([P, P], BF16, name="ones")
+        nc.vector.memset(ones[:], 1.0)
+        brow = keep.tile([P, OUT_F], BF16, name="brow")
+        nc.vector.memset(brow[:].bitcast(I32), 0)
+        nc.scalar.dma_start(out=brow[0:1, :], in_=bias.rearrange("(o f) -> o f", o=1))
+
+        x_view = x_in.rearrange("(a p e) k -> a p (e k)", a=4, p=P, e=2)
+        x_sb = [keep.tile([P, 2 * IN_F], BF16, name="x_sb%d" % a) for a in range(4)]
+        w_sb = keep.tile([P, 4, OUT_F], BF16, name="w_sb")
+        a_view = adj.rearrange("(m p) j -> m p j", p=P)
+        a_sb = [keep.tile([P, NODES], BF16, name="a_sb%d" % m) for m in range(8)]
+        nc.sync.dma_start(out=x_sb[0][:], in_=x_view[0])
+        nc.sync.dma_start(
+            out=w_sb[:].rearrange("p (u e) c -> p u (e c)", u=2),
+            in_=weight.rearrange("(u p e) c -> p u (e c)", u=2, p=P, e=2),
+        )
+        for a in range(1, 4):
+            nc.sync.dma_start(out=x_sb[a][:], in_=x_view[a])
+        for m in range(8):
+            nc.sync.dma_start(out=a_sb[m][:], in_=a_view[m])
+
+        w_grp = keep.tile([P, OUT_F, 4], BF16, name="w_grp", align_bytes=64)
+        w_cod = keep.tile([P, OUT_F], U32, name="w_cod", align_bytes=64)
+        w_scl = keep.tile([P, OUT_F], U8, name="w_scl", align_bytes=64)
+        for h in range(2):
+            cols = slice(h * 256, (h + 1) * 256)
+            nc.vector.tensor_copy(
+                out=w_grp[:, cols, :].rearrange("p (c i) t -> p c t i", i=4),
+                in_=w_sb[:, :, cols].rearrange("p t (c i) -> p c t i", i=4),
+            )
+        for h in range(2):
+            cols = slice(h * 256, (h + 1) * 256)
+            nc.vector.quantize_mx(
+                out=w_cod[:, cols].bitcast(FP8X4),
+                scales=w_scl[:, cols],
+                in_=w_grp[:, cols, :].rearrange("p c t -> p (c t)"),
+            )
+
+        x_grp = [keep.tile([P, 1024], BF16, name="x_grp%d" % a, align_bytes=64) for a in range(4)]
+        x_cod = [keep.tile([P, 256], U32, name="x_cod%d" % a, align_bytes=64) for a in range(4)]
+        x_scl = [keep.tile([P, 256], U8, name="x_scl%d" % a, align_bytes=64) for a in range(4)]
+
+        def do_x(a):
+            xt = ps_t.tile([P, 512], F32, name="xt", tag="tp")
+            xf = x_sb[a][:].bitcast(F32)
+            for u in range(2):
+                for e in range(2):
+                    nc.tensor.transpose(
+                        xt[:, (2 * u + e) * P : (2 * u + e + 1) * P],
+                        xf[:, e * 256 + u * P : e * 256 + (u + 1) * P],
+                        ident[:],
+                    )
+            nc.scalar.copy(
+                out=x_grp[a][:].bitcast(F32).rearrange("p (n u) -> p n u", u=2),
+                in_=xt[:].rearrange("p (u n) -> p n u", u=2),
+            )
+            nc.vector.quantize_mx(
+                out=x_cod[a][:].bitcast(FP8X4), scales=x_scl[a][:], in_=x_grp[a][:]
+            )
+
+        s_grp = [keep.tile([P, 2048], BF16, name="s_grp%d" % g, align_bytes=64) for g in range(2)]
+        s_cod = [keep.tile([P, 512], U32, name="s_cod%d" % g, align_bytes=64) for g in range(2)]
+        s_scl = [keep.tile([P, 512], U8, name="s_scl%d" % g, align_bytes=64) for g in range(2)]
+
+        def do_support(g):
+            for c in range(4):
+                sp = ps_s.tile([P, 512], F32, name="sp", tag="sp")
+                for t in range(4):
+                    a, e = 2 * g + t // 2, t % 2
+                    nc.tensor.matmul_mx(
+                        out=sp[:, t * P : (t + 1) * P],
+                        lhsT=x_cod[a][:, e * P : (e + 1) * P].bitcast(FP8X4),
+                        lhsT_scale=x_scl[a][:, e * P : (e + 1) * P],
+                        rhs=w_cod[:, c * P : (c + 1) * P].bitcast(FP8X4),
+                        rhs_scale=w_scl[:, c * P : (c + 1) * P],
+                        start=True,
+                        stop=True,
+                    )
+                dst = s_grp[g][:, c * 512 : (c + 1) * 512].rearrange("p (f t) -> p f t", t=4)
+                src = sp[:].rearrange("p (t f) -> p f t", t=4)
+                if c % 2 == 0:
+                    nc.scalar.copy(out=dst, in_=src)
+                else:
+                    nc.vector.tensor_copy(out=dst, in_=src)
+            nc.vector.quantize_mx(
+                out=s_cod[g][:].bitcast(FP8X4), scales=s_scl[g][:], in_=s_grp[g][:]
+            )
+
+        do_x(0)
+        do_x(1)
+
+        bp = ps_t.tile([P, 512], F32, name="bp", tag="tp")
+        nc.tensor.matmul(out=bp[:], lhsT=ones[:], rhs=brow[:], start=True, stop=True)
+        bias_sb = keep.tile([P, OUT_F], F32, name="bias_sb")
+        nc.vector.tensor_copy(out=bias_sb[:], in_=bp[:])
+
+        do_support(0)
+        do_x(2)
+        do_x(3)
+        do_support(1)
+
+        o_view = out.rearrange("(m p) f -> m p f", p=P)
+        for m in range(8):
+            at = ps_t.tile([P, 512], F32, name="at", tag="tp")
+            af = a_sb[m][:].bitcast(F32)
+            for g in range(2):
+                for u in range(2):
+                    nc.tensor.transpose(
+                        at[:, (2 * u + g) * P : (2 * u + g + 1) * P],
+                        af[:, (2 * g + u) * P : (2 * g + u + 1) * P],
+                        ident[:],
+                    )
+            k_grp = keep.tile([P, 1024], BF16, name="k_grp%d" % m, align_bytes=64)
+            k_cod = keep.tile([P, 256], U32, name="k_cod%d" % m, align_bytes=64)
+            k_scl = keep.tile([P, 256], U8, name="k_scl%d" % m, align_bytes=64)
+            nc.scalar.activation(
+                out=k_grp[:].rearrange("p (q u e) -> p q u e", u=2, e=2),
+                in_=at[:].bitcast(BF16).rearrange("p (u q e) -> p q u e", u=2, e=2),
+                func=ACT.Square,
+            )
+            nc.vector.quantize_mx(out=k_cod[:].bitcast(FP8X4), scales=k_scl[:], in_=k_grp[:])
+
+            acc = ps_o.tile([P, 512], F32, name="acc", tag="acc")
+            for g in range(2):
+                nc.tensor.matmul_mx(
+                    out=acc[:],
+                    lhsT=k_cod[:, g * P : (g + 1) * P].bitcast(FP8X4),
+                    lhsT_scale=k_scl[:, g * P : (g + 1) * P],
+                    rhs=s_cod[g][:].bitcast(FP8X4),
+                    rhs_scale=s_scl[g][:],
+                    start=(g == 0),
+                    stop=(g == 1),
+                )
+            v = keep.tile([P, OUT_F], F32, name="v%d" % m)
+            ex = keep.tile([P, OUT_F], F32, name="ex%d" % m)
+            nc.vector.tensor_tensor(out=v[:], in0=acc[:], in1=bias_sb[:], op=ALU.add)
+            nc.scalar.activation(out=ex[:], in_=v[:], func=ACT.Exp)
+            nc.vector.tensor_scalar(
+                out=ex[:], in0=ex[:], scalar1=1.0, scalar2=-1.0, op0=ALU.min, op1=ALU.add
+            )
+            nc.vector.tensor_tensor(out=v[:], in0=v[:], in1=ex[:], op=ALU.max)
+            nc.sync.dma_start(out=o_view[m], in_=v[:])

@@ -18,14 +18,33 @@ IN_F = 512
 OUT_F = 512
 FLOPS = 2 * NODES * IN_F * OUT_F + 2 * NODES * NODES * OUT_F
 
+PINNED = True
+LOADS = ["W","X0","X1","X2","X3","A0","A1","A2","A3","A4","A5","A6","A7"]
+ORDER = ["RW0","TX0","RW1","EX0","TX1","QW0","QW1","EX1","TX2","QX0","TX3","EX2","QX1","TA0","EX3","QX2","M1_00","M1_01","SQ0","QX3","TA1","ES_00","M1_02","M1_03","ES_01","SQ1","TA2","ES_02","M1_10","M1_11","ES_03","TA3","SQ2","M1_12","ES_10","M1_13","BM","QS0","SQ3","TA4","TA5","ES_11","TA6","ES_12","TA7","BE","ES_13","SQ4","QK0","QS1","SQ5","QK1","M2_0","QK2","QK3","M2_1","QK4","SQ6","A0","M2_2","QK5","M2_3","A1","SQ7","M2_4","QK6","A2","M2_5","X0","QK7","M2_6","A3","X1","M2_7","A4","X2","C0","C1","A5","X3","A6","C2","D0","A7","X4","ST0","D1","C3","D2","X5","ST1","C4","X6","ST2","D3","C5","D4","ST3","X7","D5","ST4","C6","ST5","C7","D6","D7","ST6","ST7"]
+X_ENG = ["ACT","ACT","ACT","ACT"]
+S_ENG = ["DVE","DVE","DVE","DVE","DVE","DVE","DVE","DVE"]
+B_ENG = "ACT"
+K_ENG = ["ACT","ACT","ACT","ACT","ACT","ACT","ACT","ACT"]
+FORM = [1,2,2,2,1,2,2,2]
+
 
 def tile_netgraphconvolution_kernel(tc, x_in, adj, weight, bias, out):
     nc = tc.nc
     with ExitStack() as ctx:
         keep = ctx.enter_context(tc.tile_pool(name="keep", bufs=1))
-        ps_t = ctx.enter_context(tc.psum_pool(name="ps_t", bufs=3))
-        ps_s = ctx.enter_context(tc.psum_pool(name="ps_s", bufs=2))
-        ps_o = ctx.enter_context(tc.psum_pool(name="ps_o", bufs=3))
+        psum = ctx.enter_context(tc.psum_pool(name="psum", bufs=8))
+        banks = {}
+
+        def bank(key):
+            t = psum.tile([P, 512], F32, name="bank", tag="bank")
+            banks[key] = t
+            return t
+
+        def copy_on(eng, dst, src):
+            if eng == "ACT":
+                nc.scalar.copy(out=dst, in_=src)
+            else:
+                nc.vector.tensor_copy(out=dst, in_=src)
 
         ident = keep.tile([P, P], F32, name="ident")
         make_identity(nc, ident[:])
@@ -43,26 +62,45 @@ def tile_netgraphconvolution_kernel(tc, x_in, adj, weight, bias, out):
         w_sb = keep.tile([P, 4, OUT_F], BF16, name="w_sb")
         a_view = adj.rearrange("(m p) j -> m p j", p=P)
         a_sb = [keep.tile([P, NODES], BF16, name="a_sb%d" % m) for m in range(8)]
-        nc.sync.dma_start(out=x_sb[0][:], in_=x_view[0])
-        nc.sync.dma_start(
-            out=w_sb[:].rearrange("p (u e) c -> p u (e c)", u=2),
-            in_=weight.rearrange("(u p e) c -> p u (e c)", u=2, p=P, e=2),
-        )
-        for a in range(1, 4):
-            nc.sync.dma_start(out=x_sb[a][:], in_=x_view[a])
-        for m in range(8):
-            nc.sync.dma_start(out=a_sb[m][:], in_=a_view[m])
+        o_view = out.rearrange("(m p) f -> m p f", p=P)
+        w_view = weight.rearrange("(u p e) c -> p u e c", u=2, p=P, e=2)
+        for ld in LOADS:
+            i = int(ld[1:]) if len(ld) > 1 else 0
+            if ld == "W":
+                nc.sync.dma_start(
+                    out=w_sb[:].rearrange("p (u e) c -> p u (e c)", u=2),
+                    in_=w_view.rearrange("p u e c -> p u (e c)"),
+                )
+            elif ld[0] == "X":
+                nc.sync.dma_start(out=x_sb[i][:], in_=x_view[i])
+            else:
+                nc.sync.dma_start(out=a_sb[i][:], in_=a_view[i])
 
         w_grp = keep.tile([P, OUT_F, 4], BF16, name="w_grp", align_bytes=64)
         w_cod = keep.tile([P, OUT_F], U32, name="w_cod", align_bytes=64)
         w_scl = keep.tile([P, OUT_F], U8, name="w_scl", align_bytes=64)
-        for h in range(2):
+        x_grp = [keep.tile([P, 1024], BF16, name="x_grp%d" % a, align_bytes=64) for a in range(4)]
+        x_cod = [keep.tile([P, 256], U32, name="x_cod%d" % a, align_bytes=64) for a in range(4)]
+        x_scl = [keep.tile([P, 256], U8, name="x_scl%d" % a, align_bytes=64) for a in range(4)]
+        s_grp = [keep.tile([P, 2048], BF16, name="s_grp%d" % g, align_bytes=64) for g in range(2)]
+        s_cod = [keep.tile([P, 512], U32, name="s_cod%d" % g, align_bytes=64) for g in range(2)]
+        s_scl = [keep.tile([P, 512], U8, name="s_scl%d" % g, align_bytes=64) for g in range(2)]
+        k_raw = [keep.tile([P, 1024], BF16, name="k_raw%d" % m, align_bytes=64) for m in range(8)]
+        k_grp = [keep.tile([P, 1024], BF16, name="k_grp%d" % m, align_bytes=64) for m in range(8)]
+        k_cod = [keep.tile([P, 256], U32, name="k_cod%d" % m, align_bytes=64) for m in range(8)]
+        k_scl = [keep.tile([P, 256], U8, name="k_scl%d" % m, align_bytes=64) for m in range(8)]
+        bias_sb = keep.tile([P, OUT_F], F32, name="bias_sb")
+        v = [keep.tile([P, OUT_F], F32, name="v%d" % m) for m in range(8)]
+        ex = [keep.tile([P, OUT_F], F32, name="ex%d" % m) for m in range(8)]
+
+        def op_rw(h):
             cols = slice(h * 256, (h + 1) * 256)
             nc.vector.tensor_copy(
                 out=w_grp[:, cols, :].rearrange("p (c i) t -> p c t i", i=4),
                 in_=w_sb[:, :, cols].rearrange("p t (c i) -> p c t i", i=4),
             )
-        for h in range(2):
+
+        def op_qw(h):
             cols = slice(h * 256, (h + 1) * 256)
             nc.vector.quantize_mx(
                 out=w_cod[:, cols].bitcast(FP8X4),
@@ -70,12 +108,8 @@ def tile_netgraphconvolution_kernel(tc, x_in, adj, weight, bias, out):
                 in_=w_grp[:, cols, :].rearrange("p c t -> p (c t)"),
             )
 
-        x_grp = [keep.tile([P, 1024], BF16, name="x_grp%d" % a, align_bytes=64) for a in range(4)]
-        x_cod = [keep.tile([P, 256], U32, name="x_cod%d" % a, align_bytes=64) for a in range(4)]
-        x_scl = [keep.tile([P, 256], U8, name="x_scl%d" % a, align_bytes=64) for a in range(4)]
-
-        def do_x(a):
-            xt = ps_t.tile([P, 512], F32, name="xt", tag="tp")
+        def op_tx(a):
+            xt = bank("X%d" % a)
             xf = x_sb[a][:].bitcast(F32)
             for u in range(2):
                 for e in range(2):
@@ -84,58 +118,53 @@ def tile_netgraphconvolution_kernel(tc, x_in, adj, weight, bias, out):
                         xf[:, e * 256 + u * P : e * 256 + (u + 1) * P],
                         ident[:],
                     )
-            nc.scalar.copy(
-                out=x_grp[a][:].bitcast(F32).rearrange("p (n u) -> p n u", u=2),
-                in_=xt[:].rearrange("p (u n) -> p n u", u=2),
+
+        def op_ex(a):
+            copy_on(
+                X_ENG[a],
+                x_grp[a][:].bitcast(F32).rearrange("p (n u) -> p n u", u=2),
+                banks["X%d" % a][:].rearrange("p (u n) -> p n u", u=2),
             )
+
+        def op_qx(a):
             nc.vector.quantize_mx(
                 out=x_cod[a][:].bitcast(FP8X4), scales=x_scl[a][:], in_=x_grp[a][:]
             )
 
-        s_grp = [keep.tile([P, 2048], BF16, name="s_grp%d" % g, align_bytes=64) for g in range(2)]
-        s_cod = [keep.tile([P, 512], U32, name="s_cod%d" % g, align_bytes=64) for g in range(2)]
-        s_scl = [keep.tile([P, 512], U8, name="s_scl%d" % g, align_bytes=64) for g in range(2)]
+        def op_bm():
+            nc.tensor.matmul(out=bank("B")[:], lhsT=ones[:], rhs=brow[:], start=True, stop=True)
 
-        def do_support(g):
-            for c in range(4):
-                sp = ps_s.tile([P, 512], F32, name="sp", tag="sp")
-                for t in range(4):
-                    a, e = 2 * g + t // 2, t % 2
-                    nc.tensor.matmul_mx(
-                        out=sp[:, t * P : (t + 1) * P],
-                        lhsT=x_cod[a][:, e * P : (e + 1) * P].bitcast(FP8X4),
-                        lhsT_scale=x_scl[a][:, e * P : (e + 1) * P],
-                        rhs=w_cod[:, c * P : (c + 1) * P].bitcast(FP8X4),
-                        rhs_scale=w_scl[:, c * P : (c + 1) * P],
-                        start=True,
-                        stop=True,
-                    )
-                dst = s_grp[g][:, c * 512 : (c + 1) * 512].rearrange("p (f t) -> p f t", t=4)
-                src = sp[:].rearrange("p (t f) -> p f t", t=4)
-                if c % 2 == 0:
-                    nc.scalar.copy(out=dst, in_=src)
-                else:
-                    nc.vector.tensor_copy(out=dst, in_=src)
+        def op_be():
+            copy_on(B_ENG, bias_sb[:], banks["B"][:])
+
+        def op_m1(g, c):
+            sp = bank("S%d%d" % (g, c))
+            for t in range(4):
+                a, e = 2 * g + t // 2, t % 2
+                nc.tensor.matmul_mx(
+                    out=sp[:, t * P : (t + 1) * P],
+                    lhsT=x_cod[a][:, e * P : (e + 1) * P].bitcast(FP8X4),
+                    lhsT_scale=x_scl[a][:, e * P : (e + 1) * P],
+                    rhs=w_cod[:, c * P : (c + 1) * P].bitcast(FP8X4),
+                    rhs_scale=w_scl[:, c * P : (c + 1) * P],
+                    start=True,
+                    stop=True,
+                )
+
+        def op_es(g, c):
+            copy_on(
+                S_ENG[4 * g + c],
+                s_grp[g][:, c * 512 : (c + 1) * 512].rearrange("p (f t) -> p f t", t=4),
+                banks["S%d%d" % (g, c)][:].rearrange("p (t f) -> p f t", t=4),
+            )
+
+        def op_qs(g):
             nc.vector.quantize_mx(
                 out=s_cod[g][:].bitcast(FP8X4), scales=s_scl[g][:], in_=s_grp[g][:]
             )
 
-        do_x(0)
-        do_x(1)
-
-        bp = ps_t.tile([P, 512], F32, name="bp", tag="tp")
-        nc.tensor.matmul(out=bp[:], lhsT=ones[:], rhs=brow[:], start=True, stop=True)
-        bias_sb = keep.tile([P, OUT_F], F32, name="bias_sb")
-        nc.vector.tensor_copy(out=bias_sb[:], in_=bp[:])
-
-        do_support(0)
-        do_x(2)
-        do_x(3)
-        do_support(1)
-
-        o_view = out.rearrange("(m p) f -> m p f", p=P)
-        for m in range(8):
-            at = ps_t.tile([P, 512], F32, name="at", tag="tp")
+        def op_ta(m):
+            at = bank("A%d" % m)
             af = a_sb[m][:].bitcast(F32)
             for g in range(2):
                 for u in range(2):
@@ -144,33 +173,87 @@ def tile_netgraphconvolution_kernel(tc, x_in, adj, weight, bias, out):
                         af[:, (2 * g + u) * P : (2 * g + u + 1) * P],
                         ident[:],
                     )
-            k_grp = keep.tile([P, 1024], BF16, name="k_grp%d" % m, align_bytes=64)
-            k_cod = keep.tile([P, 256], U32, name="k_cod%d" % m, align_bytes=64)
-            k_scl = keep.tile([P, 256], U8, name="k_scl%d" % m, align_bytes=64)
-            nc.scalar.activation(
-                out=k_grp[:].rearrange("p (q u e) -> p q u e", u=2, e=2),
-                in_=at[:].bitcast(BF16).rearrange("p (u q e) -> p q u e", u=2, e=2),
-                func=ACT.Square,
-            )
-            nc.vector.quantize_mx(out=k_cod[:].bitcast(FP8X4), scales=k_scl[:], in_=k_grp[:])
 
-            acc = ps_o.tile([P, 512], F32, name="acc", tag="acc")
+        def op_ck(m):
+            nc.vector.tensor_copy(
+                out=k_raw[m][:].bitcast(F32).rearrange("p (q u) -> p q u", u=2),
+                in_=banks["A%d" % m][:].rearrange("p (u q) -> p q u", u=2),
+            )
+
+        def op_sq(m):
+            if K_ENG[m] == "ACT":
+                nc.scalar.activation(
+                    out=k_grp[m][:].rearrange("p (q u e) -> p q u e", u=2, e=2),
+                    in_=banks["A%d" % m][:].bitcast(BF16).rearrange("p (u q e) -> p q u e", u=2, e=2),
+                    func=ACT.Square,
+                )
+            else:
+                nc.vector.tensor_tensor(out=k_grp[m][:], in0=k_raw[m][:], in1=k_raw[m][:], op=ALU.mult)
+
+        def op_qk(m):
+            nc.vector.quantize_mx(
+                out=k_cod[m][:].bitcast(FP8X4), scales=k_scl[m][:], in_=k_grp[m][:]
+            )
+
+        def op_m2(m):
+            acc = bank("O%d" % m)
             for g in range(2):
                 nc.tensor.matmul_mx(
                     out=acc[:],
-                    lhsT=k_cod[:, g * P : (g + 1) * P].bitcast(FP8X4),
-                    lhsT_scale=k_scl[:, g * P : (g + 1) * P],
+                    lhsT=k_cod[m][:, g * P : (g + 1) * P].bitcast(FP8X4),
+                    lhsT_scale=k_scl[m][:, g * P : (g + 1) * P],
                     rhs=s_cod[g][:].bitcast(FP8X4),
                     rhs_scale=s_scl[g][:],
                     start=(g == 0),
                     stop=(g == 1),
                 )
-            v = keep.tile([P, OUT_F], F32, name="v%d" % m)
-            ex = keep.tile([P, OUT_F], F32, name="ex%d" % m)
-            nc.vector.tensor_tensor(out=v[:], in0=acc[:], in1=bias_sb[:], op=ALU.add)
-            nc.scalar.activation(out=ex[:], in_=v[:], func=ACT.Exp)
-            nc.vector.tensor_scalar(
-                out=ex[:], in0=ex[:], scalar1=1.0, scalar2=-1.0, op0=ALU.min, op1=ALU.add
-            )
-            nc.vector.tensor_tensor(out=v[:], in0=v[:], in1=ex[:], op=ALU.max)
-            nc.sync.dma_start(out=o_view[m], in_=v[:])
+
+        def op_a(m):
+            nc.vector.tensor_tensor(out=v[m][:], in0=banks["O%d" % m][:], in1=bias_sb[:], op=ALU.add)
+
+        def op_x(m):
+            nc.scalar.activation(out=ex[m][:], in_=v[m][:], func=ACT.Exp)
+
+        def op_c(m):
+            if FORM[m] == 1:
+                nc.vector.tensor_scalar(
+                    out=ex[m][:], in0=ex[m][:], scalar1=1.0, scalar2=-1.0, op0=ALU.min, op1=ALU.add
+                )
+            else:
+                nc.scalar.activation(out=ex[m][:], in_=ex[m][:], func=ACT.Relu, bias=1.0, scale=-1.0)
+
+        def op_d(m):
+            if FORM[m] == 1:
+                nc.vector.tensor_tensor(out=v[m][:], in0=v[m][:], in1=ex[m][:], op=ALU.max)
+            else:
+                nc.vector.scalar_tensor_tensor(
+                    out=v[m][:], in0=v[m][:], scalar=0.0, in1=ex[m][:], op0=ALU.max, op1=ALU.subtract
+                )
+
+        def op_st(m):
+            nc.sync.dma_start(out=o_view[m], in_=v[m][:])
+
+        one = {"RW": op_rw, "QW": op_qw, "TX": op_tx, "EX": op_ex, "QX": op_qx, "QS": op_qs,
+               "TA": op_ta, "CK": op_ck, "SQ": op_sq, "QK": op_qk, "A": op_a, "X": op_x,
+               "C": op_c, "D": op_d, "ST": op_st}
+
+        def emit():
+            for name in ORDER:
+                if name == "BM":
+                    op_bm()
+                elif name == "BE":
+                    op_be()
+                elif name[:3] == "M1_":
+                    op_m1(int(name[3]), int(name[4]))
+                elif name[:3] == "ES_":
+                    op_es(int(name[3]), int(name[4]))
+                elif name[:3] == "M2_":
+                    op_m2(int(name[3]))
+                else:
+                    one[name[:-1]](int(name[-1]))
+
+        if PINNED:
+            with tc.manual_schedule():
+                emit()
+        else:
+            emit()

@@ -20,12 +20,12 @@ FLOPS = 2 * NODES * IN_F * OUT_F + 2 * NODES * NODES * OUT_F
 
 PINNED = True
 LOADS = ["W","X0","X1","X2","X3","A0","A1","A2","A3","A4","A5","A6","A7"]
-ORDER = ["RW0","TX0","RW1","EX0","TX1","QW0","QW1","EX1","TX2","QX0","TX3","EX2","QX1","TA0","EX3","QX2","M1_00","M1_01","SQ0","QX3","TA1","ES_00","M1_02","M1_03","ES_01","SQ1","TA2","ES_02","M1_10","M1_11","ES_03","TA3","SQ2","M1_12","ES_10","M1_13","BM","QS0","SQ3","TA4","TA5","ES_11","TA6","ES_12","TA7","BE","ES_13","SQ4","QK0","QS1","SQ5","QK1","M2_0","QK2","QK3","M2_1","QK4","SQ6","A0","M2_2","QK5","M2_3","A1","SQ7","M2_4","QK6","A2","M2_5","X0","QK7","M2_6","A3","X1","M2_7","A4","X2","C0","C1","A5","X3","A6","C2","D0","A7","X4","ST0","D1","C3","D2","X5","ST1","C4","X6","ST2","D3","C5","D4","ST3","X7","D5","ST4","C6","ST5","C7","D6","D7","ST6","ST7"]
+ORDER = ["RW0","TX0","RW1","EX0","TX1","QW0","QW1","EX1","TX2","QX0","BM","EX2","TX3","QX1","BE","TA0","EX3","M1_00","QX2","M1_01","SQ0","QX3","TA1","ES_00","M1_02","M1_03","ES_01","SQ1","M1_11","TA2","ES_02","M1_10","ES_03","M1_12","ES_11","TA3","QK0","M1_13","SQ2","ES_10","TA4","TA5","ES_12","TA6","SQ3","QK1","TA7","ES_13","QS0","SQ4","QS1","QK2","SQ5","M2_0","QK3","QK4","M2_1","A0","SQ6","M2_2","A1","M2_3","QK5","A2","X0","M2_4","QK6","M2_5","SQ7","A3","C0","M2_6","X1","QK7","D0","X2","M2_7","A4","C1","ST0","X3","A5","C2","X4","A6","X5","C3","A7","C4","D1","X6","D2","ST1","X7","D3","ST2","C5","D4","ST3","C6","D5","ST4","C7","D6","ST5","D7","ST6","ST7"]
 X_ENG = ["ACT","ACT","ACT","ACT"]
-S_ENG = ["DVE","DVE","DVE","DVE","DVE","DVE","DVE","DVE"]
-B_ENG = "ACT"
+S_ENG = ["DVE","DVE","DVE","DVE","DVE","ACT","DVE","DVE"]
+B_ENG = "DVE"
 K_ENG = ["ACT","ACT","ACT","ACT","ACT","ACT","ACT","ACT"]
-FORM = [1,2,2,2,1,2,2,2]
+FORM = [3,3,3,3,2,2,2,2]
 
 
 def tile_netgraphconvolution_kernel(tc, x_in, adj, weight, bias, out):
@@ -47,15 +47,9 @@ def tile_netgraphconvolution_kernel(tc, x_in, adj, weight, bias, out):
                 nc.vector.tensor_copy(out=dst, in_=src)
 
         ident = keep.tile([P, P], F32, name="ident")
-        make_identity(nc, ident[:])
         warm = keep.tile([P, 1], F32, name="warm")
-        nc.vector.memset(warm[:], 0.0)
-        nc.scalar.activation(out=warm[:], in_=warm[:], func=ACT.Exp)
         ones = keep.tile([P, P], BF16, name="ones")
-        nc.vector.memset(ones[:], 1.0)
         brow = keep.tile([P, OUT_F], BF16, name="brow")
-        nc.vector.memset(brow[:].bitcast(I32), 0)
-        nc.scalar.dma_start(out=brow[0:1, :], in_=bias.rearrange("(o f) -> o f", o=1))
 
         x_view = x_in.rearrange("(a p e) k -> a p (e k)", a=4, p=P, e=2)
         x_sb = [keep.tile([P, 2 * IN_F], BF16, name="x_sb%d" % a) for a in range(4)]
@@ -64,17 +58,25 @@ def tile_netgraphconvolution_kernel(tc, x_in, adj, weight, bias, out):
         a_sb = [keep.tile([P, NODES], BF16, name="a_sb%d" % m) for m in range(8)]
         o_view = out.rearrange("(m p) f -> m p f", p=P)
         w_view = weight.rearrange("(u p e) c -> p u e c", u=2, p=P, e=2)
-        for ld in LOADS:
-            i = int(ld[1:]) if len(ld) > 1 else 0
-            if ld == "W":
-                nc.sync.dma_start(
-                    out=w_sb[:].rearrange("p (u e) c -> p u (e c)", u=2),
-                    in_=w_view.rearrange("p u e c -> p u (e c)"),
-                )
-            elif ld[0] == "X":
-                nc.sync.dma_start(out=x_sb[i][:], in_=x_view[i])
-            else:
-                nc.sync.dma_start(out=a_sb[i][:], in_=a_view[i])
+        def head():
+            nc.vector.memset(brow[:].bitcast(I32), 0)
+            nc.scalar.dma_start(out=brow[0:1, :], in_=bias.rearrange("(o f) -> o f", o=1))
+            for ld in LOADS:
+                i = int(ld[1:]) if len(ld) > 1 else 0
+                if ld == "W":
+                    nc.sync.dma_start(
+                        out=w_sb[:].rearrange("p (u e) c -> p u (e c)", u=2),
+                        in_=w_view.rearrange("p u e c -> p u (e c)"),
+                    )
+                elif ld[0] == "X":
+                    nc.sync.dma_start(out=x_sb[i][:], in_=x_view[i])
+                else:
+                    nc.sync.dma_start(out=a_sb[i][:], in_=a_view[i])
+
+            make_identity(nc, ident[:])
+            nc.vector.memset(ones[:], 1.0)
+            nc.vector.memset(warm[:], 0.0)
+            nc.scalar.activation(out=warm[:], in_=warm[:], func=ACT.Exp)
 
         w_grp = keep.tile([P, OUT_F, 4], BF16, name="w_grp", align_bytes=64)
         w_cod = keep.tile([P, OUT_F], U32, name="w_cod", align_bytes=64)
@@ -217,18 +219,19 @@ def tile_netgraphconvolution_kernel(tc, x_in, adj, weight, bias, out):
         def op_c(m):
             if FORM[m] == 1:
                 nc.vector.tensor_scalar(
-                    out=ex[m][:], in0=ex[m][:], scalar1=1.0, scalar2=-1.0, op0=ALU.min, op1=ALU.add
+                    out=ex[m][:], in0=ex[m][:], scalar1=-1.0, scalar2=None, op0=ALU.add
                 )
+            elif FORM[m] == 2:
+                nc.scalar.activation(out=ex[m][:], in_=ex[m][:], func=ACT.Identity, bias=-1.0, scale=1.0)
             else:
-                nc.scalar.activation(out=ex[m][:], in_=ex[m][:], func=ACT.Relu, bias=1.0, scale=-1.0)
+                nc.gpsimd.tensor_scalar(
+                    out=ex[m][:], in0=ex[m][:], scalar1=-1.0, scalar2=1.0, op0=ALU.add, op1=ALU.mult
+                )
 
         def op_d(m):
-            if FORM[m] == 1:
-                nc.vector.tensor_tensor(out=v[m][:], in0=v[m][:], in1=ex[m][:], op=ALU.max)
-            else:
-                nc.vector.scalar_tensor_tensor(
-                    out=v[m][:], in0=v[m][:], scalar=0.0, in1=ex[m][:], op0=ALU.max, op1=ALU.subtract
-                )
+            nc.vector.scalar_tensor_tensor(
+                out=v[m][:], in0=v[m][:], scalar=0.0, in1=ex[m][:], op0=ALU.max, op1=ALU.min
+            )
 
         def op_st(m):
             nc.sync.dma_start(out=o_view[m], in_=v[m][:])
@@ -254,6 +257,8 @@ def tile_netgraphconvolution_kernel(tc, x_in, adj, weight, bias, out):
 
         if PINNED:
             with tc.manual_schedule():
+                head()
                 emit()
         else:
+            head()
             emit()

@@ -19,10 +19,10 @@ OUT_F = 512
 FLOPS = 2 * NODES * IN_F * OUT_F + 2 * NODES * NODES * OUT_F
 
 PINNED = True
-LOADS = ["W","X0","X1","X2","X3","A0","A1","A2","A3","A4","A5","A6","A7"]
-ORDER = ["RW0","TX0","RW1","EX0","TX1","QW0","QW1","EX1","TX2","QX0","BM","EX2","TX3","QX1","BE","TA0","EX3","M1_00","QX2","M1_01","SQ0","QX3","TA1","ES_00","M1_02","M1_03","ES_01","SQ1","M1_11","TA2","ES_02","M1_10","ES_03","M1_12","ES_11","TA3","QK0","M1_13","SQ2","ES_10","TA4","TA5","ES_12","TA6","SQ3","QK1","TA7","ES_13","QS0","SQ4","QS1","QK2","SQ5","M2_0","QK3","QK4","M2_1","A0","SQ6","M2_2","A1","M2_3","QK5","A2","X0","M2_4","QK6","M2_5","SQ7","A3","C0","M2_6","X1","QK7","D0","X2","M2_7","A4","C1","ST0","X3","A5","C2","X4","A6","X5","C3","A7","C4","D1","X6","D2","ST1","X7","D3","ST2","C5","D4","ST3","C6","D5","ST4","C7","D6","ST5","D7","ST6","ST7"]
+LOADS = ["A0","W","X0","X1","X2","X3","A1","A2","A3","A4","A5","A6","A7"]
+ORDER = ["TA0","SQ0","RW0","TX0","RW1","EX0","TX1","QW0","BM","QW1","EX1","TX2","QX0","BE","TX3","EX2","QX1","TA1","EX3","QX2","M1_00","QK0","SQ1","M1_01","QX3","TA2","ES_00","M1_02","ES_01","M1_03","SQ2","TA3","ES_02","M1_10","M1_11","ES_03","SQ3","M1_12","M1_13","ES_10","TA4","ES_11","TA5","ES_13","TA6","QK1","TA7","SQ4","ES_12","QS0","SQ5","QS1","QK2","M2_0","QK3","SQ6","QK4","M2_1","A0","M2_2","A1","X0","M2_3","QK5","SQ7","A2","C0","M2_4","M2_5","QK6","X1","A3","M2_6","X2","QK7","D0","M2_7","X3","A4","C1","ST0","A5","X4","C2","A6","X5","C3","A7","C4","D1","X6","D2","ST1","X7","D3","ST2","C5","D4","ST3","C6","D5","ST4","C7","D6","ST5","D7","ST6","ST7"]
 X_ENG = ["ACT","ACT","ACT","ACT"]
-S_ENG = ["DVE","DVE","DVE","DVE","DVE","ACT","DVE","DVE"]
+S_ENG = ["DVE","DVE","DVE","DVE","DVE","DVE","DVE","ACT"]
 B_ENG = "DVE"
 K_ENG = ["ACT","ACT","ACT","ACT","ACT","ACT","ACT","ACT"]
 FORM = [3,3,3,3,2,2,2,2]

@@ -19,11 +19,11 @@ OUT_F = 512
 FLOPS = 2 * NODES * IN_F * OUT_F + 2 * NODES * NODES * OUT_F
 
 PINNED = True
-LOADS = ["A0","W","X0","X1","X2","X3","A1","A2","A3","A4","A5","A6","A7"]
-ORDER = ["TA0","SQ0","RW0","TX0","RW1","EX0","TX1","QW0","BM","QW1","EX1","TX2","QX0","BE","TX3","EX2","QX1","TA1","EX3","QX2","M1_00","QK0","SQ1","M1_01","QX3","TA2","ES_00","M1_02","ES_01","M1_03","SQ2","TA3","ES_02","M1_10","M1_11","ES_03","SQ3","M1_12","M1_13","ES_10","TA4","ES_11","TA5","ES_13","TA6","QK1","TA7","SQ4","ES_12","QS0","SQ5","QS1","QK2","M2_0","QK3","SQ6","QK4","M2_1","A0","M2_2","A1","X0","M2_3","QK5","SQ7","A2","C0","M2_4","M2_5","QK6","X1","A3","M2_6","X2","QK7","D0","M2_7","X3","A4","C1","ST0","A5","X4","C2","A6","X5","C3","A7","C4","D1","X6","D2","ST1","X7","D3","ST2","C5","D4","ST3","C6","D5","ST4","C7","D6","ST5","D7","ST6","ST7"]
+LOADS = ["W","X0","X1","X2","X3","A0","A1","A2","A3","A4","A5","A6","A7"]
+ORDER = ["RW0","TX0","RW1","EX0","TX1","QW0","QW1","EX1","TX2","QX0","TX3","EX2","QX1","BM","TA0","EX3","QX2","M1_00","BE","M1_01","QX3","TA1","ES_00","SQ0","M1_02","ES_01","M1_03","M1_11","ES_02","TA2","SQ1","M1_10","ES_03","M1_12","TA3","QK0","ES_11","ES_10","M1_13","TA4","SQ2","ES_12","TA5","TA6","QK1","ES_13","SQ3","TA7","QS0","QS1","SQ4","QK2","M2_0","QK3","SQ5","M2_1","QK4","A0","M2_2","A1","SQ6","M2_3","QK5","M2_4","A2","M2_5","X0","QK6","A3","SQ7","M2_6","C0","X1","QK7","D0","X2","M2_7","A4","C1","ST0","X3","A5","C2","X4","A6","X5","C3","A7","C4","D1","X6","D2","ST1","C5","D3","ST2","X7","D4","ST3","C6","D5","ST4","C7","D6","ST5","D7","ST6","ST7"]
 X_ENG = ["ACT","ACT","ACT","ACT"]
-S_ENG = ["DVE","DVE","DVE","DVE","DVE","DVE","DVE","ACT"]
-B_ENG = "DVE"
+S_ENG = ["DVE","DVE","DVE","DVE","DVE","ACT","DVE","DVE"]
+B_ENG = "ACT"
 K_ENG = ["ACT","ACT","ACT","ACT","ACT","ACT","ACT","ACT"]
 FORM = [3,3,3,3,2,2,2,2]
 

@@ -13,19 +13,20 @@ ALU = mybir.AluOpType
 ACT = mybir.ActivationFunctionType
 
 P = 128
+PACK = 4
+BANK = 512
 NODES = 1024
 IN_F = 512
 OUT_F = 512
-FLOPS = 2 * NODES * IN_F * OUT_F + 2 * NODES * NODES * OUT_F
+ADJ_TILES = NODES // P
+X_CHUNKS = NODES // (2 * P)
+PASSES = NODES // (P * PACK)
+F_BLOCKS = OUT_F // P
 
-PINNED = True
-LOADS = ["W","X0","X1","X2","X3","A0","A1","A2","A3","A4","A5","A6","A7"]
-ORDER = ["RW0","TX0","RW1","EX0","TX1","QW0","QW1","EX1","TX2","QX0","TX3","EX2","QX1","BM","TA0","EX3","QX2","M1_00","BE","M1_01","QX3","TA1","ES_00","SQ0","M1_02","ES_01","M1_03","M1_11","ES_02","TA2","SQ1","M1_10","ES_03","M1_12","TA3","QK0","ES_11","ES_10","M1_13","TA4","SQ2","ES_12","TA5","TA6","QK1","ES_13","SQ3","TA7","QS0","QS1","SQ4","QK2","M2_0","QK3","SQ5","M2_1","QK4","A0","M2_2","A1","SQ6","M2_3","QK5","M2_4","A2","M2_5","X0","QK6","A3","SQ7","M2_6","C0","X1","QK7","D0","X2","M2_7","A4","C1","ST0","X3","A5","C2","X4","A6","X5","C3","A7","C4","D1","X6","D2","ST1","C5","D3","ST2","X7","D4","ST3","C6","D5","ST4","C7","D6","ST5","D7","ST6","ST7"]
-X_ENG = ["ACT","ACT","ACT","ACT"]
-S_ENG = ["DVE","DVE","DVE","DVE","DVE","ACT","DVE","DVE"]
-B_ENG = "ACT"
-K_ENG = ["ACT","ACT","ACT","ACT","ACT","ACT","ACT","ACT"]
-FORM = [3,3,3,3,2,2,2,2]
+SCALAR_EXIT = (1, 0)
+GPSIMD_TILES = 4
+
+FLOPS = 2 * NODES * IN_F * OUT_F + 2 * NODES * NODES * OUT_F
 
 
 def tile_netgraphconvolution_kernel(tc, x_in, adj, weight, bias, out):
@@ -33,118 +34,90 @@ def tile_netgraphconvolution_kernel(tc, x_in, adj, weight, bias, out):
     with ExitStack() as ctx:
         keep = ctx.enter_context(tc.tile_pool(name="keep", bufs=1))
         psum = ctx.enter_context(tc.psum_pool(name="psum", bufs=8))
-        banks = {}
+        ctx.enter_context(tc.manual_schedule())
 
-        def bank(key):
-            t = psum.tile([P, 512], F32, name="bank", tag="bank")
-            banks[key] = t
-            return t
-
-        def copy_on(eng, dst, src):
-            if eng == "ACT":
-                nc.scalar.copy(out=dst, in_=src)
-            else:
-                nc.vector.tensor_copy(out=dst, in_=src)
+        x_view = x_in.rearrange("(a p e) k -> a p (e k)", a=X_CHUNKS, p=P, e=2)
+        w_view = weight.rearrange("(u p e) c -> p u (e c)", u=2, p=P, e=2)
+        a_view = adj.rearrange("(m p) j -> m p j", p=P)
+        o_view = out.rearrange("(m p) f -> m p f", p=P)
 
         ident = keep.tile([P, P], F32, name="ident")
-        warm = keep.tile([P, 1], F32, name="warm")
         ones = keep.tile([P, P], BF16, name="ones")
-        brow = keep.tile([P, OUT_F], BF16, name="brow")
-
-        x_view = x_in.rearrange("(a p e) k -> a p (e k)", a=4, p=P, e=2)
-        x_sb = [keep.tile([P, 2 * IN_F], BF16, name="x_sb%d" % a) for a in range(4)]
-        w_sb = keep.tile([P, 4, OUT_F], BF16, name="w_sb")
-        a_view = adj.rearrange("(m p) j -> m p j", p=P)
-        a_sb = [keep.tile([P, NODES], BF16, name="a_sb%d" % m) for m in range(8)]
-        o_view = out.rearrange("(m p) f -> m p f", p=P)
-        w_view = weight.rearrange("(u p e) c -> p u e c", u=2, p=P, e=2)
-        def head():
-            nc.vector.memset(brow[:].bitcast(I32), 0)
-            nc.scalar.dma_start(out=brow[0:1, :], in_=bias.rearrange("(o f) -> o f", o=1))
-            for ld in LOADS:
-                i = int(ld[1:]) if len(ld) > 1 else 0
-                if ld == "W":
-                    nc.sync.dma_start(
-                        out=w_sb[:].rearrange("p (u e) c -> p u (e c)", u=2),
-                        in_=w_view.rearrange("p u e c -> p u (e c)"),
-                    )
-                elif ld[0] == "X":
-                    nc.sync.dma_start(out=x_sb[i][:], in_=x_view[i])
-                else:
-                    nc.sync.dma_start(out=a_sb[i][:], in_=a_view[i])
-
-            make_identity(nc, ident[:])
-            nc.vector.memset(ones[:], 1.0)
-            nc.vector.memset(warm[:], 0.0)
-            nc.scalar.activation(out=warm[:], in_=warm[:], func=ACT.Exp)
-
-        w_grp = keep.tile([P, OUT_F, 4], BF16, name="w_grp", align_bytes=64)
+        bias_row = keep.tile([P, OUT_F], BF16, name="bias_row")
+        bias_all = keep.tile([P, OUT_F], F32, name="bias_all")
+        warm = keep.tile([P, 1], F32, name="warm")
+        w_raw = keep.tile([P, PACK, OUT_F], BF16, name="w_raw")
+        x_raw = [keep.tile([P, 2 * IN_F], BF16, name="x_raw%d" % a) for a in range(X_CHUNKS)]
+        a_raw = [keep.tile([P, NODES], BF16, name="a_raw%d" % m) for m in range(ADJ_TILES)]
+        w_grp = keep.tile([P, OUT_F, PACK], BF16, name="w_grp", align_bytes=64)
         w_cod = keep.tile([P, OUT_F], U32, name="w_cod", align_bytes=64)
         w_scl = keep.tile([P, OUT_F], U8, name="w_scl", align_bytes=64)
-        x_grp = [keep.tile([P, 1024], BF16, name="x_grp%d" % a, align_bytes=64) for a in range(4)]
-        x_cod = [keep.tile([P, 256], U32, name="x_cod%d" % a, align_bytes=64) for a in range(4)]
-        x_scl = [keep.tile([P, 256], U8, name="x_scl%d" % a, align_bytes=64) for a in range(4)]
-        s_grp = [keep.tile([P, 2048], BF16, name="s_grp%d" % g, align_bytes=64) for g in range(2)]
-        s_cod = [keep.tile([P, 512], U32, name="s_cod%d" % g, align_bytes=64) for g in range(2)]
-        s_scl = [keep.tile([P, 512], U8, name="s_scl%d" % g, align_bytes=64) for g in range(2)]
-        k_raw = [keep.tile([P, 1024], BF16, name="k_raw%d" % m, align_bytes=64) for m in range(8)]
-        k_grp = [keep.tile([P, 1024], BF16, name="k_grp%d" % m, align_bytes=64) for m in range(8)]
-        k_cod = [keep.tile([P, 256], U32, name="k_cod%d" % m, align_bytes=64) for m in range(8)]
-        k_scl = [keep.tile([P, 256], U8, name="k_scl%d" % m, align_bytes=64) for m in range(8)]
-        bias_sb = keep.tile([P, OUT_F], F32, name="bias_sb")
-        v = [keep.tile([P, OUT_F], F32, name="v%d" % m) for m in range(8)]
-        ex = [keep.tile([P, OUT_F], F32, name="ex%d" % m) for m in range(8)]
+        x_grp = [keep.tile([P, 2 * P * PACK], BF16, name="x_grp%d" % a, align_bytes=64) for a in range(X_CHUNKS)]
+        x_cod = [keep.tile([P, 2 * P], U32, name="x_cod%d" % a, align_bytes=64) for a in range(X_CHUNKS)]
+        x_scl = [keep.tile([P, 2 * P], U8, name="x_scl%d" % a, align_bytes=64) for a in range(X_CHUNKS)]
+        s_grp = [keep.tile([P, OUT_F * PACK], BF16, name="s_grp%d" % g, align_bytes=64) for g in range(PASSES)]
+        s_cod = [keep.tile([P, OUT_F], U32, name="s_cod%d" % g, align_bytes=64) for g in range(PASSES)]
+        s_scl = [keep.tile([P, OUT_F], U8, name="s_scl%d" % g, align_bytes=64) for g in range(PASSES)]
+        k_grp = [
+            keep.tile([P, PASSES * P * PACK], BF16, name="k_grp%d" % m, align_bytes=64) for m in range(ADJ_TILES)
+        ]
+        k_cod = [keep.tile([P, PASSES * P], U32, name="k_cod%d" % m, align_bytes=64) for m in range(ADJ_TILES)]
+        k_scl = [keep.tile([P, PASSES * P], U8, name="k_scl%d" % m, align_bytes=64) for m in range(ADJ_TILES)]
+        v = [keep.tile([P, OUT_F], F32, name="v%d" % m) for m in range(ADJ_TILES)]
+        ex = [keep.tile([P, OUT_F], F32, name="ex%d" % m) for m in range(ADJ_TILES)]
 
-        def op_rw(h):
-            cols = slice(h * 256, (h + 1) * 256)
+        banks = {}
+
+        def new_bank(key):
+            banks[key] = psum.tile([P, BANK], F32, name="bank", tag="bank")
+            return banks[key]
+
+        def regroup_weight(h):
+            cols = slice(h * OUT_F // 2, (h + 1) * OUT_F // 2)
             nc.vector.tensor_copy(
                 out=w_grp[:, cols, :].rearrange("p (c i) t -> p c t i", i=4),
-                in_=w_sb[:, :, cols].rearrange("p t (c i) -> p c t i", i=4),
+                in_=w_raw[:, :, cols].rearrange("p t (c i) -> p c t i", i=4),
             )
 
-        def op_qw(h):
-            cols = slice(h * 256, (h + 1) * 256)
+        def quantise_weight(h):
+            cols = slice(h * OUT_F // 2, (h + 1) * OUT_F // 2)
             nc.vector.quantize_mx(
                 out=w_cod[:, cols].bitcast(FP8X4),
                 scales=w_scl[:, cols],
                 in_=w_grp[:, cols, :].rearrange("p c t -> p (c t)"),
             )
 
-        def op_tx(a):
-            xt = bank("X%d" % a)
-            xf = x_sb[a][:].bitcast(F32)
+        def transpose_x(a):
+            bank = new_bank(("x", a))
+            words = x_raw[a][:].bitcast(F32)
             for u in range(2):
                 for e in range(2):
                     nc.tensor.transpose(
-                        xt[:, (2 * u + e) * P : (2 * u + e + 1) * P],
-                        xf[:, e * 256 + u * P : e * 256 + (u + 1) * P],
+                        bank[:, (2 * u + e) * P : (2 * u + e + 1) * P],
+                        words[:, (2 * e + u) * P : (2 * e + u + 1) * P],
                         ident[:],
                     )
 
-        def op_ex(a):
-            copy_on(
-                X_ENG[a],
-                x_grp[a][:].bitcast(F32).rearrange("p (n u) -> p n u", u=2),
-                banks["X%d" % a][:].rearrange("p (u n) -> p n u", u=2),
+        def exit_x(a):
+            nc.scalar.copy(
+                out=x_grp[a][:].bitcast(F32).rearrange("p (n u) -> p n u", u=2),
+                in_=banks[("x", a)][:].rearrange("p (u n) -> p n u", u=2),
             )
 
-        def op_qx(a):
-            nc.vector.quantize_mx(
-                out=x_cod[a][:].bitcast(FP8X4), scales=x_scl[a][:], in_=x_grp[a][:]
-            )
+        def quantise_x(a):
+            nc.vector.quantize_mx(out=x_cod[a][:].bitcast(FP8X4), scales=x_scl[a][:], in_=x_grp[a][:])
 
-        def op_bm():
-            nc.tensor.matmul(out=bank("B")[:], lhsT=ones[:], rhs=brow[:], start=True, stop=True)
+        def spread_bias():
+            bank = new_bank("bias")
+            nc.tensor.matmul(out=bank[:], lhsT=ones[:], rhs=bias_row[:], start=True, stop=True)
+            nc.scalar.copy(out=bias_all[:], in_=bank[:])
 
-        def op_be():
-            copy_on(B_ENG, bias_sb[:], banks["B"][:])
-
-        def op_m1(g, c):
-            sp = bank("S%d%d" % (g, c))
-            for t in range(4):
+        def support_bank(g, c):
+            bank = new_bank(("s", g, c))
+            for t in range(PACK):
                 a, e = 2 * g + t // 2, t % 2
                 nc.tensor.matmul_mx(
-                    out=sp[:, t * P : (t + 1) * P],
+                    out=bank[:, t * P : (t + 1) * P],
                     lhsT=x_cod[a][:, e * P : (e + 1) * P].bitcast(FP8X4),
                     lhsT_scale=x_scl[a][:, e * P : (e + 1) * P],
                     rhs=w_cod[:, c * P : (c + 1) * P].bitcast(FP8X4),
@@ -153,112 +126,130 @@ def tile_netgraphconvolution_kernel(tc, x_in, adj, weight, bias, out):
                     stop=True,
                 )
 
-        def op_es(g, c):
-            copy_on(
-                S_ENG[4 * g + c],
-                s_grp[g][:, c * 512 : (c + 1) * 512].rearrange("p (f t) -> p f t", t=4),
-                banks["S%d%d" % (g, c)][:].rearrange("p (t f) -> p f t", t=4),
-            )
+        def exit_support(g, c):
+            dst = s_grp[g][:, c * P * PACK : (c + 1) * P * PACK].rearrange("p (f t) -> p f t", t=PACK)
+            src = banks[("s", g, c)][:].rearrange("p (t f) -> p f t", t=PACK)
+            if (g, c) == SCALAR_EXIT:
+                nc.scalar.copy(out=dst, in_=src)
+            else:
+                nc.vector.tensor_copy(out=dst, in_=src)
 
-        def op_qs(g):
-            nc.vector.quantize_mx(
-                out=s_cod[g][:].bitcast(FP8X4), scales=s_scl[g][:], in_=s_grp[g][:]
-            )
+        def quantise_support(g):
+            nc.vector.quantize_mx(out=s_cod[g][:].bitcast(FP8X4), scales=s_scl[g][:], in_=s_grp[g][:])
 
-        def op_ta(m):
-            at = bank("A%d" % m)
-            af = a_sb[m][:].bitcast(F32)
-            for g in range(2):
+        def transpose_adj(m):
+            bank = new_bank(("a", m))
+            words = a_raw[m][:].bitcast(F32)
+            for g in range(PASSES):
                 for u in range(2):
                     nc.tensor.transpose(
-                        at[:, (2 * u + g) * P : (2 * u + g + 1) * P],
-                        af[:, (2 * g + u) * P : (2 * g + u + 1) * P],
+                        bank[:, (2 * u + g) * P : (2 * u + g + 1) * P],
+                        words[:, (2 * g + u) * P : (2 * g + u + 1) * P],
                         ident[:],
                     )
 
-        def op_ck(m):
-            nc.vector.tensor_copy(
-                out=k_raw[m][:].bitcast(F32).rearrange("p (q u) -> p q u", u=2),
-                in_=banks["A%d" % m][:].rearrange("p (u q) -> p q u", u=2),
+        def square_adj(m):
+            nc.scalar.activation(
+                out=k_grp[m][:].rearrange("p (q u e) -> p q u e", u=2, e=2),
+                in_=banks[("a", m)][:].bitcast(BF16).rearrange("p (u q e) -> p q u e", u=2, e=2),
+                func=ACT.Square,
             )
 
-        def op_sq(m):
-            if K_ENG[m] == "ACT":
-                nc.scalar.activation(
-                    out=k_grp[m][:].rearrange("p (q u e) -> p q u e", u=2, e=2),
-                    in_=banks["A%d" % m][:].bitcast(BF16).rearrange("p (u q e) -> p q u e", u=2, e=2),
-                    func=ACT.Square,
-                )
-            else:
-                nc.vector.tensor_tensor(out=k_grp[m][:], in0=k_raw[m][:], in1=k_raw[m][:], op=ALU.mult)
+        def quantise_adj(m):
+            nc.vector.quantize_mx(out=k_cod[m][:].bitcast(FP8X4), scales=k_scl[m][:], in_=k_grp[m][:])
 
-        def op_qk(m):
-            nc.vector.quantize_mx(
-                out=k_cod[m][:].bitcast(FP8X4), scales=k_scl[m][:], in_=k_grp[m][:]
-            )
-
-        def op_m2(m):
-            acc = bank("O%d" % m)
-            for g in range(2):
+        def second_matmul(m):
+            bank = new_bank(("o", m))
+            for g in range(PASSES):
                 nc.tensor.matmul_mx(
-                    out=acc[:],
+                    out=bank[:],
                     lhsT=k_cod[m][:, g * P : (g + 1) * P].bitcast(FP8X4),
                     lhsT_scale=k_scl[m][:, g * P : (g + 1) * P],
                     rhs=s_cod[g][:].bitcast(FP8X4),
                     rhs_scale=s_scl[g][:],
                     start=(g == 0),
-                    stop=(g == 1),
+                    stop=(g == PASSES - 1),
                 )
 
-        def op_a(m):
-            nc.vector.tensor_tensor(out=v[m][:], in0=banks["O%d" % m][:], in1=bias_sb[:], op=ALU.add)
+        def add_bias(m):
+            nc.vector.tensor_tensor(out=v[m][:], in0=banks[("o", m)][:], in1=bias_all[:], op=ALU.add)
 
-        def op_x(m):
+        def exponential(m):
             nc.scalar.activation(out=ex[m][:], in_=v[m][:], func=ACT.Exp)
 
-        def op_c(m):
-            if FORM[m] == 1:
-                nc.vector.tensor_scalar(
-                    out=ex[m][:], in0=ex[m][:], scalar1=-1.0, scalar2=None, op0=ALU.add
-                )
-            elif FORM[m] == 2:
-                nc.scalar.activation(out=ex[m][:], in_=ex[m][:], func=ACT.Identity, bias=-1.0, scale=1.0)
-            else:
+        def minus_one(m):
+            if m < GPSIMD_TILES:
                 nc.gpsimd.tensor_scalar(
                     out=ex[m][:], in0=ex[m][:], scalar1=-1.0, scalar2=1.0, op0=ALU.add, op1=ALU.mult
                 )
+            else:
+                nc.scalar.activation(out=ex[m][:], in_=ex[m][:], func=ACT.Identity, bias=-1.0, scale=1.0)
 
-        def op_d(m):
+        def finish(m):
             nc.vector.scalar_tensor_tensor(
                 out=v[m][:], in0=v[m][:], scalar=0.0, in1=ex[m][:], op0=ALU.max, op1=ALU.min
             )
-
-        def op_st(m):
             nc.sync.dma_start(out=o_view[m], in_=v[m][:])
 
-        one = {"RW": op_rw, "QW": op_qw, "TX": op_tx, "EX": op_ex, "QX": op_qx, "QS": op_qs,
-               "TA": op_ta, "CK": op_ck, "SQ": op_sq, "QK": op_qk, "A": op_a, "X": op_x,
-               "C": op_c, "D": op_d, "ST": op_st}
 
-        def emit():
-            for name in ORDER:
-                if name == "BM":
-                    op_bm()
-                elif name == "BE":
-                    op_be()
-                elif name[:3] == "M1_":
-                    op_m1(int(name[3]), int(name[4]))
-                elif name[:3] == "ES_":
-                    op_es(int(name[3]), int(name[4]))
-                elif name[:3] == "M2_":
-                    op_m2(int(name[3]))
-                else:
-                    one[name[:-1]](int(name[-1]))
+        nc.vector.memset(bias_row[:].bitcast(I32), 0)
+        nc.scalar.dma_start(out=bias_row[0:1, :], in_=bias.rearrange("(o f) -> o f", o=1))
+        nc.sync.dma_start(out=w_raw[:].rearrange("p (u e) c -> p u (e c)", u=2), in_=w_view)
+        for a in range(X_CHUNKS):
+            nc.sync.dma_start(out=x_raw[a][:], in_=x_view[a])
+        for m in range(ADJ_TILES):
+            nc.sync.dma_start(out=a_raw[m][:], in_=a_view[m])
+        make_identity(nc, ident[:])
+        nc.vector.memset(ones[:], 1.0)
+        nc.vector.memset(warm[:], 0.0)
+        nc.scalar.activation(out=warm[:], in_=warm[:], func=ACT.Exp)
 
-        if PINNED:
-            with tc.manual_schedule():
-                head()
-                emit()
-        else:
-            head()
-            emit()
+        for h in range(2):
+            regroup_weight(h)
+        for h in range(2):
+            quantise_weight(h)
+
+        for a in range(X_CHUNKS):
+            transpose_x(a)
+            exit_x(a)
+            quantise_x(a)
+        spread_bias()
+
+        quantise_after_bank = {3: 0, 6: 1}
+        for n in range(PASSES * F_BLOCKS):
+            g, c = divmod(n, F_BLOCKS)
+            if n % 2 == 0:
+                transpose_adj(n // 2)
+            support_bank(g, c)
+            exit_support(g, c)
+            if n % 2 == 0:
+                square_adj(n // 2)
+            if n in quantise_after_bank:
+                quantise_adj(quantise_after_bank[n])
+
+        for m in range(4, ADJ_TILES):
+            transpose_adj(m)
+        for g in range(PASSES):
+            quantise_support(g)
+        for m in (4, 5, 6):
+            square_adj(m)
+        for m in (2, 3, 4):
+            quantise_adj(m)
+
+        for m in range(ADJ_TILES):
+            second_matmul(m)
+            add_bias(m)
+            exponential(m)
+            if m == 0:
+                square_adj(ADJ_TILES - 1)
+            if m < GPSIMD_TILES:
+                minus_one(m)
+            elif m > GPSIMD_TILES:
+                minus_one(m - 1)
+            if 1 <= m <= 3:
+                quantise_adj(m + 4)
+            if m == 3:
+                finish(0)
+        minus_one(ADJ_TILES - 1)
+        for m in range(1, ADJ_TILES):
+            finish(m)

@@ -215,15 +215,16 @@ def tile_netgraphconvolution_kernel(tc, x_in, adj, weight, bias, out):
             quantise_x(a)
         spread_bias()
 
+        adj_before_bank = {0: 0, 2: 1, 5: 2, 7: 3}
         quantise_after_bank = {3: 0, 6: 1}
         for n in range(PASSES * F_BLOCKS):
             g, c = divmod(n, F_BLOCKS)
-            if n % 2 == 0:
-                transpose_adj(n // 2)
+            if n in adj_before_bank:
+                transpose_adj(adj_before_bank[n])
             support_bank(g, c)
             exit_support(g, c)
-            if n % 2 == 0:
-                square_adj(n // 2)
+            if n in adj_before_bank:
+                square_adj(adj_before_bank[n])
             if n in quantise_after_bank:
                 quantise_adj(quantise_after_bank[n])
 

@@ -25,6 +25,7 @@ F_BLOCKS = OUT_F // P
 
 SCALAR_EXIT = (1, 0)
 GPSIMD_TILES = 4
+EARLY = 3
 
 FLOPS = 2 * NODES * IN_F * OUT_F + 2 * NODES * NODES * OUT_F
 
@@ -158,18 +159,17 @@ def tile_netgraphconvolution_kernel(tc, x_in, adj, weight, bias, out):
         def quantise_adj(m):
             nc.vector.quantize_mx(out=k_cod[m][:].bitcast(FP8X4), scales=k_scl[m][:], in_=k_grp[m][:])
 
-        def second_matmul(m):
-            bank = new_bank(("o", m))
-            for g in range(PASSES):
-                nc.tensor.matmul_mx(
-                    out=bank[:],
-                    lhsT=k_cod[m][:, g * P : (g + 1) * P].bitcast(FP8X4),
-                    lhsT_scale=k_scl[m][:, g * P : (g + 1) * P],
-                    rhs=s_cod[g][:].bitcast(FP8X4),
-                    rhs_scale=s_scl[g][:],
-                    start=(g == 0),
-                    stop=(g == PASSES - 1),
-                )
+        def second_matmul(m, g):
+            bank = new_bank(("o", m)) if g == 0 else banks[("o", m)]
+            nc.tensor.matmul_mx(
+                out=bank[:],
+                lhsT=k_cod[m][:, g * P : (g + 1) * P].bitcast(FP8X4),
+                lhsT_scale=k_scl[m][:, g * P : (g + 1) * P],
+                rhs=s_cod[g][:].bitcast(FP8X4),
+                rhs_scale=s_scl[g][:],
+                start=(g == 0),
+                stop=(g == PASSES - 1),
+            )
 
         def add_bias(m):
             nc.vector.tensor_tensor(out=v[m][:], in0=banks[("o", m)][:], in1=bias_all[:], op=ALU.add)
@@ -227,18 +227,27 @@ def tile_netgraphconvolution_kernel(tc, x_in, adj, weight, bias, out):
                 square_adj(adj_before_bank[n])
             if n in quantise_after_bank:
                 quantise_adj(quantise_after_bank[n])
+            if n == F_BLOCKS - 1:
+                quantise_support(0)
 
-        for m in range(4, ADJ_TILES):
+        for m in (4, 5):
             transpose_adj(m)
-        for g in range(PASSES):
-            quantise_support(g)
+        for m in (0, 1):
+            second_matmul(m, 0)
+        for m in (6, 7):
+            transpose_adj(m)
+        quantise_adj(2)
+        second_matmul(2, 0)
+        quantise_support(1)
         for m in (4, 5, 6):
             square_adj(m)
-        for m in (2, 3, 4):
+        for m in (3, 4):
             quantise_adj(m)
 
         for m in range(ADJ_TILES):
-            second_matmul(m)
+            if m >= EARLY:
+                second_matmul(m, 0)
+            second_matmul(m, 1)
             add_bias(m)
             exponential(m)
             if m == 0:

from contextlib import ExitStack

import concourse.mybir as mybir
from concourse.masks import make_identity

F32 = mybir.dt.float32
BF16 = mybir.dt.bfloat16
U32 = mybir.dt.uint32
U8 = mybir.dt.uint8
I32 = mybir.dt.int32
FP8X4 = mybir.dt.float8_e4m3fn_x4
ALU = mybir.AluOpType
ACT = mybir.ActivationFunctionType

P = 128
PACK = 4
BANK = 512
NODES = 1024
IN_F = 512
OUT_F = 512
ADJ_TILES = NODES // P
X_CHUNKS = NODES // (2 * P)
PASSES = NODES // (P * PACK)
F_BLOCKS = OUT_F // P

SCALAR_EXIT = (1, 0)
GPSIMD_TILES = 4
EARLY = 3

FLOPS = 2 * NODES * IN_F * OUT_F + 2 * NODES * NODES * OUT_F


def tile_netgraphconvolution_kernel(tc, x_in, adj, weight, bias, out):
    nc = tc.nc
    with ExitStack() as ctx:
        keep = ctx.enter_context(tc.tile_pool(name="keep", bufs=1))
        psum = ctx.enter_context(tc.psum_pool(name="psum", bufs=8))
        ctx.enter_context(tc.manual_schedule())

        x_view = x_in.rearrange("(a p e) k -> a p (e k)", a=X_CHUNKS, p=P, e=2)
        w_view = weight.rearrange("(u p e) c -> p u (e c)", u=2, p=P, e=2)
        a_view = adj.rearrange("(m p) j -> m p j", p=P)
        o_view = out.rearrange("(m p) f -> m p f", p=P)

        ident = keep.tile([P, P], F32, name="ident")
        ones = keep.tile([P, P], BF16, name="ones")
        bias_row = keep.tile([P, OUT_F], BF16, name="bias_row")
        bias_all = keep.tile([P, OUT_F], F32, name="bias_all")
        warm = keep.tile([P, 1], F32, name="warm")
        w_raw = keep.tile([P, PACK, OUT_F], BF16, name="w_raw")
        x_raw = [keep.tile([P, 2 * IN_F], BF16, name="x_raw%d" % a) for a in range(X_CHUNKS)]
        a_raw = [keep.tile([P, NODES], BF16, name="a_raw%d" % m) for m in range(ADJ_TILES)]
        w_grp = keep.tile([P, OUT_F, PACK], BF16, name="w_grp", align_bytes=64)
        w_cod = keep.tile([P, OUT_F], U32, name="w_cod", align_bytes=64)
        w_scl = keep.tile([P, OUT_F], U8, name="w_scl", align_bytes=64)
        x_grp = [keep.tile([P, 2 * P * PACK], BF16, name="x_grp%d" % a, align_bytes=64) for a in range(X_CHUNKS)]
        x_cod = [keep.tile([P, 2 * P], U32, name="x_cod%d" % a, align_bytes=64) for a in range(X_CHUNKS)]
        x_scl = [keep.tile([P, 2 * P], U8, name="x_scl%d" % a, align_bytes=64) for a in range(X_CHUNKS)]
        s_grp = [keep.tile([P, OUT_F * PACK], BF16, name="s_grp%d" % g, align_bytes=64) for g in range(PASSES)]
        s_cod = [keep.tile([P, OUT_F], U32, name="s_cod%d" % g, align_bytes=64) for g in range(PASSES)]
        s_scl = [keep.tile([P, OUT_F], U8, name="s_scl%d" % g, align_bytes=64) for g in range(PASSES)]
        k_grp = [
            keep.tile([P, PASSES * P * PACK], BF16, name="k_grp%d" % m, align_bytes=64) for m in range(ADJ_TILES)
        ]
        k_cod = [keep.tile([P, PASSES * P], U32, name="k_cod%d" % m, align_bytes=64) for m in range(ADJ_TILES)]
        k_scl = [keep.tile([P, PASSES * P], U8, name="k_scl%d" % m, align_bytes=64) for m in range(ADJ_TILES)]
        v = [keep.tile([P, OUT_F], F32, name="v%d" % m) for m in range(ADJ_TILES)]
        ex = [keep.tile([P, OUT_F], F32, name="ex%d" % m) for m in range(ADJ_TILES)]

        banks = {}

        def new_bank(key):
            banks[key] = psum.tile([P, BANK], F32, name="bank", tag="bank")
            return banks[key]

        def regroup_weight(h):
            cols = slice(h * OUT_F // 2, (h + 1) * OUT_F // 2)
            nc.vector.tensor_copy(
                out=w_grp[:, cols, :].rearrange("p (c i) t -> p c t i", i=4),
                in_=w_raw[:, :, cols].rearrange("p t (c i) -> p c t i", i=4),
            )

        def quantise_weight(h):
            cols = slice(h * OUT_F // 2, (h + 1) * OUT_F // 2)
            nc.vector.quantize_mx(
                out=w_cod[:, cols].bitcast(FP8X4),
                scales=w_scl[:, cols],
                in_=w_grp[:, cols, :].rearrange("p c t -> p (c t)"),
            )

        def transpose_x(a):
            bank = new_bank(("x", a))
            words = x_raw[a][:].bitcast(F32)
            for u in range(2):
                for e in range(2):
                    nc.tensor.transpose(
                        bank[:, (2 * u + e) * P : (2 * u + e + 1) * P],
                        words[:, (2 * e + u) * P : (2 * e + u + 1) * P],
                        ident[:],
                    )

        def exit_x(a):
            nc.scalar.copy(
                out=x_grp[a][:].bitcast(F32).rearrange("p (n u) -> p n u", u=2),
                in_=banks[("x", a)][:].rearrange("p (u n) -> p n u", u=2),
            )

        def quantise_x(a):
            nc.vector.quantize_mx(out=x_cod[a][:].bitcast(FP8X4), scales=x_scl[a][:], in_=x_grp[a][:])

        def spread_bias():
            bank = new_bank("bias")
            nc.tensor.matmul(out=bank[:], lhsT=ones[:], rhs=bias_row[:], start=True, stop=True)
            nc.scalar.copy(out=bias_all[:], in_=bank[:])

        def support_bank(g, c):
            bank = new_bank(("s", g, c))
            for t in range(PACK):
                a, e = 2 * g + t // 2, t % 2
                nc.tensor.matmul_mx(
                    out=bank[:, t * P : (t + 1) * P],
                    lhsT=x_cod[a][:, e * P : (e + 1) * P].bitcast(FP8X4),
                    lhsT_scale=x_scl[a][:, e * P : (e + 1) * P],
                    rhs=w_cod[:, c * P : (c + 1) * P].bitcast(FP8X4),
                    rhs_scale=w_scl[:, c * P : (c + 1) * P],
                    start=True,
                    stop=True,
                )

        def exit_support(g, c):
            dst = s_grp[g][:, c * P * PACK : (c + 1) * P * PACK].rearrange("p (f t) -> p f t", t=PACK)
            src = banks[("s", g, c)][:].rearrange("p (t f) -> p f t", t=PACK)
            if (g, c) == SCALAR_EXIT:
                nc.scalar.copy(out=dst, in_=src)
            else:
                nc.vector.tensor_copy(out=dst, in_=src)

        def quantise_support(g):
            nc.vector.quantize_mx(out=s_cod[g][:].bitcast(FP8X4), scales=s_scl[g][:], in_=s_grp[g][:])

        def transpose_adj(m):
            bank = new_bank(("a", m))
            words = a_raw[m][:].bitcast(F32)
            for g in range(PASSES):
                for u in range(2):
                    nc.tensor.transpose(
                        bank[:, (2 * u + g) * P : (2 * u + g + 1) * P],
                        words[:, (2 * g + u) * P : (2 * g + u + 1) * P],
                        ident[:],
                    )

        def square_adj(m):
            nc.scalar.activation(
                out=k_grp[m][:].rearrange("p (q u e) -> p q u e", u=2, e=2),
                in_=banks[("a", m)][:].bitcast(BF16).rearrange("p (u q e) -> p q u e", u=2, e=2),
                func=ACT.Square,
            )

        def quantise_adj(m):
            nc.vector.quantize_mx(out=k_cod[m][:].bitcast(FP8X4), scales=k_scl[m][:], in_=k_grp[m][:])

        def second_matmul(m, g):
            bank = new_bank(("o", m)) if g == 0 else banks[("o", m)]
            nc.tensor.matmul_mx(
                out=bank[:],
                lhsT=k_cod[m][:, g * P : (g + 1) * P].bitcast(FP8X4),
                lhsT_scale=k_scl[m][:, g * P : (g + 1) * P],
                rhs=s_cod[g][:].bitcast(FP8X4),
                rhs_scale=s_scl[g][:],
                start=(g == 0),
                stop=(g == PASSES - 1),
            )

        def add_bias(m):
            nc.vector.tensor_tensor(out=v[m][:], in0=banks[("o", m)][:], in1=bias_all[:], op=ALU.add)

        def exponential(m):
            nc.scalar.activation(out=ex[m][:], in_=v[m][:], func=ACT.Exp)

        def minus_one(m):
            if m < GPSIMD_TILES:
                nc.gpsimd.tensor_scalar(
                    out=ex[m][:], in0=ex[m][:], scalar1=-1.0, scalar2=1.0, op0=ALU.add, op1=ALU.mult
                )
            else:
                nc.scalar.activation(out=ex[m][:], in_=ex[m][:], func=ACT.Identity, bias=-1.0, scale=1.0)

        def finish(m):
            nc.vector.scalar_tensor_tensor(
                out=v[m][:], in0=v[m][:], scalar=0.0, in1=ex[m][:], op0=ALU.max, op1=ALU.min
            )
            nc.sync.dma_start(out=o_view[m], in_=v[m][:])


        nc.vector.memset(bias_row[:].bitcast(I32), 0)
        nc.scalar.dma_start(out=bias_row[0:1, :], in_=bias.rearrange("(o f) -> o f", o=1))
        nc.sync.dma_start(out=w_raw[:].rearrange("p (u e) c -> p u (e c)", u=2), in_=w_view)
        for a in range(X_CHUNKS):
            nc.sync.dma_start(out=x_raw[a][:], in_=x_view[a])
        for m in range(ADJ_TILES):
            nc.sync.dma_start(out=a_raw[m][:], in_=a_view[m])
        make_identity(nc, ident[:])
        nc.vector.memset(ones[:], 1.0)
        nc.vector.memset(warm[:], 0.0)
        nc.scalar.activation(out=warm[:], in_=warm[:], func=ACT.Exp)

        for h in range(2):
            regroup_weight(h)
        for h in range(2):
            quantise_weight(h)

        for a in range(X_CHUNKS):
            transpose_x(a)
            exit_x(a)
            quantise_x(a)
        spread_bias()

        adj_before_bank = {0: 0, 2: 1, 5: 2, 7: 3}
        quantise_after_bank = {3: 0, 6: 1}
        for n in range(PASSES * F_BLOCKS):
            g, c = divmod(n, F_BLOCKS)
            if n in adj_before_bank:
                transpose_adj(adj_before_bank[n])
            support_bank(g, c)
            exit_support(g, c)
            if n in adj_before_bank:
                square_adj(adj_before_bank[n])
            if n in quantise_after_bank:
                quantise_adj(quantise_after_bank[n])
            if n == F_BLOCKS - 1:
                quantise_support(0)

        for m in (4, 5):
            transpose_adj(m)
        for m in (0, 1):
            second_matmul(m, 0)
        for m in (6, 7):
            transpose_adj(m)
        quantise_adj(2)
        second_matmul(2, 0)
        quantise_support(1)
        for m in (4, 5, 6):
            square_adj(m)
        for m in (3, 4):
            quantise_adj(m)

        for m in range(ADJ_TILES):
            if m >= EARLY:
                second_matmul(m, 0)
            second_matmul(m, 1)
            add_bias(m)
            exponential(m)
            if m == 0:
                square_adj(ADJ_TILES - 1)
            if m < GPSIMD_TILES:
                minus_one(m)
            elif m > GPSIMD_TILES:
                minus_one(m - 1)
            if 1 <= m <= 3:
                quantise_adj(m + 4)
            if m == 3:
                finish(0)
        minus_one(ADJ_TILES - 1)
        for m in range(1, ADJ_TILES):
            finish(m)
